import numpy as np
import ml_dtypes


def mxq(x, axis, fmt="e4m3"):
    dtype, down = {"e4m3": (ml_dtypes.float8_e4m3fn, 7), "e5m2": (ml_dtypes.float8_e5m2, 14)}[fmt]
    v = np.moveaxis(np.asarray(x, np.float32).astype(ml_dtypes.bfloat16).astype(np.float64), axis, -1)
    blocks = v.reshape(v.shape[:-1] + (-1, 32))
    amax = np.abs(blocks).max(-1, keepdims=True)
    byte = np.maximum(np.where(amax > 0, np.frexp(amax)[1] - 1 + 127, 0) - down, 1)
    scale = np.exp2(byte - 127.0)
    codes = (blocks / scale).astype(np.float32).astype(dtype).astype(np.float64)
    return np.moveaxis((codes * scale).reshape(v.shape), -1, axis)


WIDE = False


def mx_kscale(k):
    if not WIDE:
        return np.ones(k)
    levels = np.array([10, -10, 5, -5, 0])
    if k % 512:
        return np.exp2(np.random.permutation(np.resize(levels, k // 32))).repeat(32)
    a = np.empty((k // 512, 16))
    for p in range(k // 512):
        a[p, :8] = np.random.permutation(np.resize(levels, 8))
        for g in range(8):
            far = levels[np.abs(levels - a[p, g]) >= 10]
            a[p, g + 8] = far[np.random.randint(len(far))]
    return np.exp2(a.ravel()).repeat(32)


BF16 = ml_dtypes.bfloat16


def bf(x):
    return np.asarray(x, np.float32).astype(BF16)


def f64(x):
    return np.asarray(x).astype(np.float64)


G, S, M, H, E, C = 2, 512, 512, 1024, 16, 64


def setup_inputs():
    s, t = mx_kscale(S), mx_kscale(M)
    return {"dispatch_mask": bf(np.random.standard_normal((G, S, E, C)) * 0.1 * s[None, :, None, None]),
            "x": bf(np.random.standard_normal((G, S, M)) / s[None, :, None] * t),
            "wi": bf(np.random.standard_normal((E, M, H)) * 10.0 / np.sqrt(S * M) / t[None, :, None])}


def reference(dispatch_mask, x, wi):
    dm = mxq(f64(dispatch_mask).reshape(G, S, E * C), 1, "e4m3")
    xq = mxq(f64(x), 1, "e4m3")
    d = f64(bf(dm.transpose(0, 2, 1) @ xq))
    dispatched = d.reshape(G, E, C, M).transpose(1, 0, 2, 3)
    pre = mxq(dispatched.reshape(E, G * C, M), 2, "e4m3") @ mxq(f64(wi), 1, "e4m3")
    return np.maximum(pre, 0.0).reshape(E, G, C, H)

@@ -1,0 +1,231 @@
+from contextlib import ExitStack
+
+import concourse.mybir as mybir
+from concourse.masks import make_identity
+
+G, S, M, H, E, C = 2, 512, 512, 1024, 16, 64
+EC = E * C
+FLOPS = 2 * G * S * EC * M + 2 * E * G * C * M * H
+
+F32 = mybir.dt.float32
+BF16 = mybir.dt.bfloat16
+U32 = mybir.dt.uint32
+U8 = mybir.dt.uint8
+FP8X4 = mybir.dt.float8_e4m3fn_x4
+RELU = mybir.ActivationFunctionType.Relu
+
+P = 128
+PACK = 4
+NB = EC // P
+HALF = 512
+BANK_DT = BF16
+X_V_SLOTS = 2
+DM_V_COLS = 352
+W_V_COLS = 608
+W_V_ONLY = 2
+LIFT_COLS = 128
+W_BUFS = 8
+BANK_BUFS = 4
+
+
+def interleave(copy, dst, src, c0, c1):
+    copy(
+        out=dst[:, c0:c1, :].rearrange("p (c i) t -> p c t i", i=4),
+        in_=src[:, :, c0:c1].rearrange("p t (c i) -> p c t i", i=4),
+    )
+
+
+def tile_flaxpositionwisemoelayer_pa_kernel(tc, dispatch_mask, x, wi, out):
+    nc = tc.nc
+    with ExitStack() as ctx:
+        keep = ctx.enter_context(tc.tile_pool(name="keep", bufs=1))
+        stream = ctx.enter_context(tc.tile_pool(name="stream", bufs=3))
+        psum1 = ctx.enter_context(tc.psum_pool(name="psum1", bufs=BANK_BUFS))
+        psum2 = ctx.enter_context(tc.psum_pool(name="psum2", bufs=4))
+
+        ident = keep.tile([P, P], BF16, name="ident")
+        make_identity(nc, ident[:])
+        warm_in = keep.tile([P, 1], F32, name="warm_in")
+        warm_out = keep.tile([P, 1], F32, name="warm_out")
+        nc.gpsimd.memset(warm_in[:], 0.0)
+        nc.scalar.activation(out=warm_out[:], in_=warm_in[:], func=RELU)
+
+        ctx.enter_context(tc.manual_schedule())
+
+        x_raw, x_grouped, x_codes, x_scales = {}, {}, {}, {}
+        dm_raw, dm_grouped, dm_codes, dm_scales = {}, {}, {}, {}
+        banks, d_grouped, d_codes, d_scales = {}, {}, {}, {}
+        w_raw, w_grouped, w_codes, w_scales, lifted = {}, {}, {}, {}, {}
+        accs, results = {}, {}
+
+        def quantize(codes, scales, grouped):
+            nc.vector.quantize_mx(out=codes.bitcast(FP8X4), scales=scales, in_=grouped)
+
+        def load_x(g):
+            x_raw[g] = keep.tile([P, PACK, M], BF16, name="x_raw%d" % g)
+            nc.sync.dma_start(out=x_raw[g][:], in_=x[g].rearrange("(p j) m -> p j m", j=PACK))
+
+        def load_dm(g, h):
+            dm_raw[g, h] = keep.tile([P, PACK, HALF], BF16, name="dm_raw%d%d" % (g, h))
+            rows = dispatch_mask[g].rearrange("(p j) e c -> p j (e c)", j=PACK)
+            nc.sync.dma_start(out=dm_raw[g, h][:], in_=rows[:, :, h * HALF : (h + 1) * HALF])
+
+        def load_w(e):
+            w_raw[e] = stream.tile([P, PACK, H], BF16, name="w_raw", bufs=W_BUFS)
+            nc.sync.dma_start(out=w_raw[e][:], in_=wi[e].rearrange("(p j) h -> p j h", j=PACK))
+
+        def group_x(g):
+            x_grouped[g] = keep.tile([P, PACK, P, PACK], BF16, name="x_grouped%d" % g, align_bytes=64)
+            src = x_raw[g][:].rearrange("p j (m t) -> p t m j", t=PACK)
+            nc.vector.tensor_copy(out=x_grouped[g][:, :X_V_SLOTS], in_=src[:, :X_V_SLOTS])
+            nc.scalar.copy(out=x_grouped[g][:, X_V_SLOTS:], in_=src[:, X_V_SLOTS:])
+
+        def quant_x(g):
+            x_codes[g] = keep.tile([P, M], U32, name="x_codes%d" % g, align_bytes=64)
+            x_scales[g] = keep.tile([P, M], U8, name="x_scales%d" % g, align_bytes=64)
+            quantize(x_codes[g][:], x_scales[g][:], x_grouped[g][:].rearrange("p t m j -> p (t m j)"))
+
+        def group_dm(g, h):
+            dm_grouped[g, h] = keep.tile([P, HALF, PACK], BF16, name="dm_grouped%d%d" % (g, h), align_bytes=64)
+            interleave(nc.vector.tensor_copy, dm_grouped[g, h], dm_raw[g, h], 0, DM_V_COLS)
+            interleave(nc.scalar.copy, dm_grouped[g, h], dm_raw[g, h], DM_V_COLS, HALF)
+
+        def quant_dm(g, h):
+            dm_codes[g, h] = keep.tile([P, HALF], U32, name="dm_codes%d%d" % (g, h), align_bytes=64)
+            dm_scales[g, h] = keep.tile([P, HALF], U8, name="dm_scales%d%d" % (g, h), align_bytes=64)
+            quantize(dm_codes[g, h][:], dm_scales[g, h][:], dm_grouped[g, h][:].rearrange("p c j -> p (c j)"))
+            ready[0] += NB // 2
+
+        def dispatch(g, b):
+            banks[g, b] = psum1.tile([P, PACK, P], BANK_DT, name="bank", tag="stage")
+            h, q = divmod(b, NB // 2)
+            for t in range(PACK):
+                nc.tensor.matmul_mx(
+                    out=banks[g, b][:, t, :],
+                    lhsT=x_codes[g][:, t * P : (t + 1) * P].bitcast(FP8X4),
+                    lhsT_scale=x_scales[g][:, t * P : (t + 1) * P],
+                    rhs=dm_codes[g, h][:, q * P : (q + 1) * P].bitcast(FP8X4),
+                    rhs_scale=dm_scales[g, h][:, q * P : (q + 1) * P],
+                    start=True,
+                    stop=True,
+                )
+
+        def empty_bank(g, b):
+            if g == 0:
+                d_grouped[b] = keep.tile([P, 2, G, C, PACK], BF16, name="d_grouped%d" % b, align_bytes=64)
+            nc.scalar.copy(
+                out=d_grouped[b][:, :, g, :, :],
+                in_=banks[g, b][:].rearrange("p t (e c) -> p e c t", e=2),
+            )
+
+        stage1 = [(g, b) for g in range(G) for b in range(NB)]
+        ready, filled, emptied = [0], [0], [0]
+
+        def fill_next():
+            if filled[0] < ready[0]:
+                dispatch(*stage1[filled[0]])
+                filled[0] += 1
+
+        def empty_next(n):
+            for i in range(n):
+                empty_bank(*stage1[emptied[0]])
+                emptied[0] += 1
+                fill_next()
+
+        def quant_d(b):
+            d_codes[b] = keep.tile([P, 2 * P], U32, name="d_codes%d" % b, align_bytes=64)
+            d_scales[b] = keep.tile([P, 2 * P], U8, name="d_scales%d" % b, align_bytes=64)
+            quantize(d_codes[b][:], d_scales[b][:], d_grouped[b][:].rearrange("p e g c t -> p (e g c t)"))
+
+        def lift(e):
+            lifted[e] = psum1.tile([P, LIFT_COLS, PACK], BF16, name="lifted", tag="stage")
+            src = w_raw[e][:, :, H - LIFT_COLS :].rearrange("p t c -> p c t")
+            nc.tensor.matmul(out=lifted[e][:], lhsT=ident[:], rhs=src, start=True, stop=True)
+
+        def group_w(e):
+            w_grouped[e] = stream.tile([P, H, PACK], BF16, name="w_grouped", align_bytes=64)
+            if e < W_V_ONLY:
+                interleave(nc.vector.tensor_copy, w_grouped[e], w_raw[e], 0, H)
+                return
+            interleave(nc.vector.tensor_copy, w_grouped[e], w_raw[e], 0, W_V_COLS)
+            interleave(nc.scalar.copy, w_grouped[e], w_raw[e], W_V_COLS, H - LIFT_COLS)
+            nc.scalar.copy(out=w_grouped[e][:, H - LIFT_COLS :, :], in_=lifted[e][:])
+
+        def quant_w(e):
+            w_codes[e] = stream.tile([P, H], U32, name="w_codes", align_bytes=64)
+            w_scales[e] = stream.tile([P, H], U8, name="w_scales", align_bytes=64)
+            quantize(w_codes[e][:], w_scales[e][:], w_grouped[e][:].rearrange("p c j -> p (c j)"))
+
+        def project(e):
+            b, half = e // 2, e % 2
+            for n in range(H // HALF):
+                accs[e, n] = psum2.tile([P, HALF], F32, name="acc")
+                nc.tensor.matmul_mx(
+                    out=accs[e, n][:],
+                    lhsT=d_codes[b][:, half * P : (half + 1) * P].bitcast(FP8X4),
+                    lhsT_scale=d_scales[b][:, half * P : (half + 1) * P],
+                    rhs=w_codes[e][:, n * HALF : (n + 1) * HALF].bitcast(FP8X4),
+                    rhs_scale=w_scales[e][:, n * HALF : (n + 1) * HALF],
+                    start=True,
+                    stop=True,
+                )
+
+        def relu_store(e):
+            results[e] = stream.tile([P, H], F32, name="result", bufs=6)
+            rows = out[e].rearrange("g c h -> (g c) h")
+            if e < E - 1:
+                for n in range(H // HALF):
+                    nc.scalar.activation(out=results[e][:, n * HALF : (n + 1) * HALF], in_=accs[e, n][:], func=RELU)
+                nc.sync.dma_start(out=rows, in_=results[e][:])
+            else:
+                nc.scalar.activation(out=results[e][:, :HALF], in_=accs[e, 0][:], func=RELU)
+                nc.vector.tensor_scalar_max(out=results[e][:, HALF:], in0=accs[e, 1][:], scalar1=0.0)
+                nc.sync.dma_start(out=rows[:, :HALF], in_=results[e][:, :HALF])
+                nc.sync.dma_start(out=rows[:, HALF:], in_=results[e][:, HALF:])
+
+        load_x(0)
+        load_x(1)
+        for g in range(G):
+            for h in range(2):
+                load_dm(g, h)
+        for e in range(W_BUFS):
+            load_w(e)
+
+        group_x(0)
+        group_x(1)
+        quant_x(0)
+        group_dm(0, 0)
+        quant_x(1)
+        group_dm(0, 1)
+        quant_dm(0, 0)
+        for i in range(BANK_BUFS):
+            fill_next()
+        group_dm(1, 0)
+        quant_dm(0, 1)
+        empty_next(2)
+        group_dm(1, 1)
+        quant_dm(1, 0)
+        empty_next(2)
+        group_w(0)
+        quant_dm(1, 1)
+        empty_next(4)
+        group_w(1)
+        quant_w(0)
+        empty_next(8)
+        lift(2)
+        for e in range(1, E):
+            if e + 2 < E:
+                lift(e + 2)
+            if e + 1 < E:
+                group_w(e + 1)
+            if e - 1 + W_BUFS < E:
+                load_w(e - 1 + W_BUFS)
+            if e == 1:
+                quant_d(0)
+                project(0)
+            if e % 2 == 0:
+                quant_d(e // 2)
+            quant_w(e)
+            project(e)
+            relu_store(e - 1)
+        relu_store(E - 1)

@@ -65,10 +65,9 @@ def tile_flaxpositionwisemoelayer_pa_kernel(tc, dispatch_mask, x, wi, out):
             x_raw[g] = keep.tile([P, PACK, M], BF16, name="x_raw%d" % g)
             nc.sync.dma_start(out=x_raw[g][:], in_=x[g].rearrange("(p j) m -> p j m", j=PACK))
 
-        def load_dm(g, h):
-            dm_raw[g, h] = keep.tile([P, PACK, HALF], BF16, name="dm_raw%d%d" % (g, h))
-            rows = dispatch_mask[g].rearrange("(p j) e c -> p j (e c)", j=PACK)
-            nc.sync.dma_start(out=dm_raw[g, h][:], in_=rows[:, :, h * HALF : (h + 1) * HALF])
+        def load_dm(g):
+            dm_raw[g] = keep.tile([P, PACK, EC], BF16, name="dm_raw%d" % g)
+            nc.sync.dma_start(out=dm_raw[g][:], in_=dispatch_mask[g].rearrange("(p j) e c -> p j (e c)", j=PACK))
 
         def load_w(e):
             w_raw[e] = stream.tile([P, PACK, H], BF16, name="w_raw", bufs=W_BUFS)
@@ -87,8 +86,9 @@ def tile_flaxpositionwisemoelayer_pa_kernel(tc, dispatch_mask, x, wi, out):
 
         def group_dm(g, h):
             dm_grouped[g, h] = keep.tile([P, HALF, PACK], BF16, name="dm_grouped%d%d" % (g, h), align_bytes=64)
-            interleave(nc.vector.tensor_copy, dm_grouped[g, h], dm_raw[g, h], 0, DM_V_COLS)
-            interleave(nc.scalar.copy, dm_grouped[g, h], dm_raw[g, h], DM_V_COLS, HALF)
+            src = dm_raw[g][:, :, h * HALF : (h + 1) * HALF]
+            interleave(nc.vector.tensor_copy, dm_grouped[g, h], src, 0, DM_V_COLS)
+            interleave(nc.scalar.copy, dm_grouped[g, h], src, DM_V_COLS, HALF)
 
         def quant_dm(g, h):
             dm_codes[g, h] = keep.tile([P, HALF], U32, name="dm_codes%d%d" % (g, h), align_bytes=64)
@@ -183,25 +183,24 @@ def tile_flaxpositionwisemoelayer_pa_kernel(tc, dispatch_mask, x, wi, out):
                 nc.sync.dma_start(out=rows[:, :HALF], in_=results[e][:, :HALF])
                 nc.sync.dma_start(out=rows[:, HALF:], in_=results[e][:, HALF:])
 
-        load_x(0)
-        load_x(1)
         for g in range(G):
-            for h in range(2):
-                load_dm(g, h)
+            load_x(g)
+            load_dm(g)
         for e in range(W_BUFS):
             load_w(e)
 
         group_x(0)
-        group_x(1)
         quant_x(0)
         group_dm(0, 0)
-        quant_x(1)
         group_dm(0, 1)
         quant_dm(0, 0)
         for i in range(BANK_BUFS):
             fill_next()
-        group_dm(1, 0)
+        group_x(1)
         quant_dm(0, 1)
+        empty_next(2)
+        group_dm(1, 0)
+        quant_x(1)
         empty_next(2)
         group_dm(1, 1)
         quant_dm(1, 0)
@@ -211,7 +210,7 @@ def tile_flaxpositionwisemoelayer_pa_kernel(tc, dispatch_mask, x, wi, out):
         empty_next(4)
         group_w(1)
         quant_w(0)
-        empty_next(8)
+        empty_next(6)
         lift(2)
         for e in range(1, E):
             if e + 2 < E:

@@ -26,12 +26,13 @@ W_V_ONLY = 2
 LIFT_COLS = 128
 W_BUFS = 8
 BANK_BUFS = 4
+RUN = 2
 
 
 def interleave(copy, dst, src, c0, c1):
     copy(
-        out=dst[:, c0:c1, :].rearrange("p (c i) t -> p c t i", i=4),
-        in_=src[:, :, c0:c1].rearrange("p t (c i) -> p c t i", i=4),
+        out=dst[:, c0:c1, :].rearrange("p (c i) t -> p c t i", i=RUN),
+        in_=src[:, :, c0:c1].rearrange("p t (c i) -> p c t i", i=RUN),
     )
 
 

@@ -21,9 +21,10 @@ HALF = 512
 BANK_DT = BF16
 X_V_SLOTS = 2
 DM_V_COLS = 352
-W_V_COLS = 608
+W_V_COLS = 576
 W_V_ONLY = 2
-LIFT_COLS = 128
+LIFT_COLS = 172
+LIFT_STEP = 128
 W_BUFS = 8
 BANK_BUFS = 4
 RUN = 2
@@ -141,7 +142,9 @@ def tile_flaxpositionwisemoelayer_pa_kernel(tc, dispatch_mask, x, wi, out):
         def lift(e):
             lifted[e] = psum1.tile([P, LIFT_COLS, PACK], BF16, name="lifted", tag="stage")
             src = w_raw[e][:, :, H - LIFT_COLS :].rearrange("p t c -> p c t")
-            nc.tensor.matmul(out=lifted[e][:], lhsT=ident[:], rhs=src, start=True, stop=True)
+            for c0 in range(0, LIFT_COLS, LIFT_STEP):
+                c1 = min(c0 + LIFT_STEP, LIFT_COLS)
+                nc.tensor.matmul(out=lifted[e][:, c0:c1, :], lhsT=ident[:], rhs=src[:, c0:c1, :], start=True, stop=True)
 
         def group_w(e):
             w_grouped[e] = stream.tile([P, H, PACK], BF16, name="w_grouped", align_bytes=64)

@@ -25,7 +25,8 @@ W_V_COLS = 576
 W_V_ONLY = 2
 LIFT_COLS = 172
 LIFT_STEP = 128
-W_BUFS = 8
+W_PAIR_BUFS = 4
+PAIRED = 12
 BANK_BUFS = 4
 RUN = 2
 
@@ -58,7 +59,7 @@ def tile_flaxpositionwisemoelayer_pa_kernel(tc, dispatch_mask, x, wi, out):
         dm_raw, dm_grouped, dm_codes, dm_scales = {}, {}, {}, {}
         banks, d_grouped, d_codes, d_scales = {}, {}, {}, {}
         w_raw, w_grouped, w_codes, w_scales, lifted = {}, {}, {}, {}, {}
-        accs, results = {}, {}
+        accs, results, result_pairs = {}, {}, {}
 
         def quantize(codes, scales, grouped):
             nc.vector.quantize_mx(out=codes.bitcast(FP8X4), scales=scales, in_=grouped)
@@ -71,9 +72,14 @@ def tile_flaxpositionwisemoelayer_pa_kernel(tc, dispatch_mask, x, wi, out):
             dm_raw[g] = keep.tile([P, PACK, EC], BF16, name="dm_raw%d" % g)
             nc.sync.dma_start(out=dm_raw[g][:], in_=dispatch_mask[g].rearrange("(p j) e c -> p j (e c)", j=PACK))
 
-        def load_w(e):
-            w_raw[e] = stream.tile([P, PACK, H], BF16, name="w_raw", bufs=W_BUFS)
-            nc.sync.dma_start(out=w_raw[e][:], in_=wi[e].rearrange("(p j) h -> p j h", j=PACK))
+        def load_w_pair(q):
+            pair = stream.tile([P, 2, PACK, H], BF16, name="w_raw", bufs=W_PAIR_BUFS)
+            w_raw[2 * q], w_raw[2 * q + 1] = pair[:, 0], pair[:, 1]
+            if q == 0:
+                for a in range(2):
+                    nc.sync.dma_start(out=pair[:, a], in_=wi[a].rearrange("(p j) h -> p j h", j=PACK))
+            else:
+                nc.sync.dma_start(out=pair[:], in_=wi[2 * q : 2 * q + 2].rearrange("e (p j) h -> p e j h", j=PACK))
 
         def group_x(g):
             x_grouped[g] = keep.tile([P, PACK, P, PACK], BF16, name="x_grouped%d" % g, align_bytes=64)
@@ -175,12 +181,17 @@ def tile_flaxpositionwisemoelayer_pa_kernel(tc, dispatch_mask, x, wi, out):
                 )
 
         def relu_store(e):
-            results[e] = stream.tile([P, H], F32, name="result", bufs=6)
+            if e % 2 == 0:
+                result_pairs[e // 2] = stream.tile([P, 2, H], F32, name="result", bufs=3)
+            results[e] = result_pairs[e // 2][:, e % 2]
             rows = out[e].rearrange("g c h -> (g c) h")
             if e < E - 1:
                 for n in range(H // HALF):
                     nc.scalar.activation(out=results[e][:, n * HALF : (n + 1) * HALF], in_=accs[e, n][:], func=RELU)
-                nc.sync.dma_start(out=rows, in_=results[e][:])
+                if e >= PAIRED:
+                    nc.sync.dma_start(out=rows, in_=results[e])
+                elif e % 2 == 1:
+                    nc.sync.dma_start(out=out[e - 1 : e + 1].rearrange("e g c h -> (g c) e h"), in_=result_pairs[e // 2][:])
             else:
                 nc.scalar.activation(out=results[e][:, :HALF], in_=accs[e, 0][:], func=RELU)
                 nc.vector.tensor_scalar_max(out=results[e][:, HALF:], in0=accs[e, 1][:], scalar1=0.0)
@@ -190,8 +201,8 @@ def tile_flaxpositionwisemoelayer_pa_kernel(tc, dispatch_mask, x, wi, out):
         for g in range(G):
             load_x(g)
             load_dm(g)
-        for e in range(W_BUFS):
-            load_w(e)
+        for q in range(W_PAIR_BUFS):
+            load_w_pair(q)
 
         group_x(0)
         quant_x(0)
@@ -221,8 +232,8 @@ def tile_flaxpositionwisemoelayer_pa_kernel(tc, dispatch_mask, x, wi, out):
                 lift(e + 2)
             if e + 1 < E:
                 group_w(e + 1)
-            if e - 1 + W_BUFS < E:
-                load_w(e - 1 + W_BUFS)
+            if e % 2 == 1 and (e - 1) // 2 + W_PAIR_BUFS < E // 2:
+                load_w_pair((e - 1) // 2 + W_PAIR_BUFS)
             if e == 1:
                 quant_d(0)
                 project(0)

@@ -21,20 +21,21 @@ HALF = 512
 BANK_DT = BF16
 X_V_SLOTS = 2
 DM_V_COLS = 352
-W_V_COLS = 576
+W_V_COLS = 580
 W_V_ONLY = 2
 LIFT_COLS = 172
 LIFT_STEP = 128
 W_PAIR_BUFS = 4
 PAIRED = 12
 BANK_BUFS = 4
-RUN = 2
+V_RUN = 2
+S_RUN = 4
 
 
-def interleave(copy, dst, src, c0, c1):
+def interleave(copy, run, dst, src, c0, c1):
     copy(
-        out=dst[:, c0:c1, :].rearrange("p (c i) t -> p c t i", i=RUN),
-        in_=src[:, :, c0:c1].rearrange("p t (c i) -> p c t i", i=RUN),
+        out=dst[:, c0:c1, :].rearrange("p (c i) t -> p c t i", i=run),
+        in_=src[:, :, c0:c1].rearrange("p t (c i) -> p c t i", i=run),
     )
 
 
@@ -95,8 +96,8 @@ def tile_flaxpositionwisemoelayer_pa_kernel(tc, dispatch_mask, x, wi, out):
         def group_dm(g, h):
             dm_grouped[g, h] = keep.tile([P, HALF, PACK], BF16, name="dm_grouped%d%d" % (g, h), align_bytes=64)
             src = dm_raw[g][:, :, h * HALF : (h + 1) * HALF]
-            interleave(nc.vector.tensor_copy, dm_grouped[g, h], src, 0, DM_V_COLS)
-            interleave(nc.scalar.copy, dm_grouped[g, h], src, DM_V_COLS, HALF)
+            interleave(nc.vector.tensor_copy, V_RUN, dm_grouped[g, h], src, 0, DM_V_COLS)
+            interleave(nc.scalar.copy, S_RUN, dm_grouped[g, h], src, DM_V_COLS, HALF)
 
         def quant_dm(g, h):
             dm_codes[g, h] = keep.tile([P, HALF], U32, name="dm_codes%d%d" % (g, h), align_bytes=64)
@@ -155,10 +156,10 @@ def tile_flaxpositionwisemoelayer_pa_kernel(tc, dispatch_mask, x, wi, out):
         def group_w(e):
             w_grouped[e] = stream.tile([P, H, PACK], BF16, name="w_grouped", align_bytes=64)
             if e < W_V_ONLY:
-                interleave(nc.vector.tensor_copy, w_grouped[e], w_raw[e], 0, H)
+                interleave(nc.vector.tensor_copy, V_RUN, w_grouped[e], w_raw[e], 0, H)
                 return
-            interleave(nc.vector.tensor_copy, w_grouped[e], w_raw[e], 0, W_V_COLS)
-            interleave(nc.scalar.copy, w_grouped[e], w_raw[e], W_V_COLS, H - LIFT_COLS)
+            interleave(nc.vector.tensor_copy, V_RUN, w_grouped[e], w_raw[e], 0, W_V_COLS)
+            interleave(nc.scalar.copy, S_RUN, w_grouped[e], w_raw[e], W_V_COLS, H - LIFT_COLS)
             nc.scalar.copy(out=w_grouped[e][:, H - LIFT_COLS :, :], in_=lifted[e][:])
 
         def quant_w(e):

@@ -27,6 +27,7 @@ LIFT_COLS = 172
 LIFT_STEP = 128
 W_PAIR_BUFS = 4
 PAIRED = 12
+DMA_ALIGN = 256
 BANK_BUFS = 4
 V_RUN = 2
 S_RUN = 4
@@ -66,15 +67,15 @@ def tile_flaxpositionwisemoelayer_pa_kernel(tc, dispatch_mask, x, wi, out):
             nc.vector.quantize_mx(out=codes.bitcast(FP8X4), scales=scales, in_=grouped)
 
         def load_x(g):
-            x_raw[g] = keep.tile([P, PACK, M], BF16, name="x_raw%d" % g)
+            x_raw[g] = keep.tile([P, PACK, M], BF16, name="x_raw%d" % g, align_bytes=DMA_ALIGN)
             nc.sync.dma_start(out=x_raw[g][:], in_=x[g].rearrange("(p j) m -> p j m", j=PACK))
 
         def load_dm(g):
-            dm_raw[g] = keep.tile([P, PACK, EC], BF16, name="dm_raw%d" % g)
+            dm_raw[g] = keep.tile([P, PACK, EC], BF16, name="dm_raw%d" % g, align_bytes=DMA_ALIGN)
             nc.sync.dma_start(out=dm_raw[g][:], in_=dispatch_mask[g].rearrange("(p j) e c -> p j (e c)", j=PACK))
 
         def load_w_pair(q):
-            pair = stream.tile([P, 2, PACK, H], BF16, name="w_raw", bufs=W_PAIR_BUFS)
+            pair = stream.tile([P, 2, PACK, H], BF16, name="w_raw", bufs=W_PAIR_BUFS, align_bytes=DMA_ALIGN)
             w_raw[2 * q], w_raw[2 * q + 1] = pair[:, 0], pair[:, 1]
             if q == 0:
                 for a in range(2):
@@ -183,7 +184,7 @@ def tile_flaxpositionwisemoelayer_pa_kernel(tc, dispatch_mask, x, wi, out):
 
         def relu_store(e):
             if e % 2 == 0:
-                result_pairs[e // 2] = stream.tile([P, 2, H], F32, name="result", bufs=3)
+                result_pairs[e // 2] = stream.tile([P, 2, H], F32, name="result", bufs=3, align_bytes=DMA_ALIGN)
             results[e] = result_pairs[e // 2][:, e % 2]
             rows = out[e].rearrange("g c h -> (g c) h")
             if e < E - 1:

from contextlib import ExitStack

import concourse.mybir as mybir
from concourse.masks import make_identity

G, S, M, H, E, C = 2, 512, 512, 1024, 16, 64
EC = E * C
FLOPS = 2 * G * S * EC * M + 2 * E * G * C * M * H

F32 = mybir.dt.float32
BF16 = mybir.dt.bfloat16
U32 = mybir.dt.uint32
U8 = mybir.dt.uint8
FP8X4 = mybir.dt.float8_e4m3fn_x4
RELU = mybir.ActivationFunctionType.Relu

P = 128
PACK = 4
NB = EC // P
HALF = 512
BANK_DT = BF16
X_V_SLOTS = 2
DM_V_COLS = 352
W_V_COLS = 580
W_V_ONLY = 2
LIFT_COLS = 172
LIFT_STEP = 128
W_PAIR_BUFS = 4
PAIRED = 12
DMA_ALIGN = 256
BANK_BUFS = 4
V_RUN = 2
S_RUN = 4


def interleave(copy, run, dst, src, c0, c1):
    copy(
        out=dst[:, c0:c1, :].rearrange("p (c i) t -> p c t i", i=run),
        in_=src[:, :, c0:c1].rearrange("p t (c i) -> p c t i", i=run),
    )


def tile_flaxpositionwisemoelayer_pa_kernel(tc, dispatch_mask, x, wi, out):
    nc = tc.nc
    with ExitStack() as ctx:
        keep = ctx.enter_context(tc.tile_pool(name="keep", bufs=1))
        stream = ctx.enter_context(tc.tile_pool(name="stream", bufs=3))
        psum1 = ctx.enter_context(tc.psum_pool(name="psum1", bufs=BANK_BUFS))
        psum2 = ctx.enter_context(tc.psum_pool(name="psum2", bufs=4))

        ident = keep.tile([P, P], BF16, name="ident")
        make_identity(nc, ident[:])
        warm_in = keep.tile([P, 1], F32, name="warm_in")
        warm_out = keep.tile([P, 1], F32, name="warm_out")
        nc.gpsimd.memset(warm_in[:], 0.0)
        nc.scalar.activation(out=warm_out[:], in_=warm_in[:], func=RELU)

        ctx.enter_context(tc.manual_schedule())

        x_raw, x_grouped, x_codes, x_scales = {}, {}, {}, {}
        dm_raw, dm_grouped, dm_codes, dm_scales = {}, {}, {}, {}
        banks, d_grouped, d_codes, d_scales = {}, {}, {}, {}
        w_raw, w_grouped, w_codes, w_scales, lifted = {}, {}, {}, {}, {}
        accs, results, result_pairs = {}, {}, {}

        def quantize(codes, scales, grouped):
            nc.vector.quantize_mx(out=codes.bitcast(FP8X4), scales=scales, in_=grouped)

        def load_x(g):
            x_raw[g] = keep.tile([P, PACK, M], BF16, name="x_raw%d" % g, align_bytes=DMA_ALIGN)
            nc.sync.dma_start(out=x_raw[g][:], in_=x[g].rearrange("(p j) m -> p j m", j=PACK))

        def load_dm(g):
            dm_raw[g] = keep.tile([P, PACK, EC], BF16, name="dm_raw%d" % g, align_bytes=DMA_ALIGN)
            nc.sync.dma_start(out=dm_raw[g][:], in_=dispatch_mask[g].rearrange("(p j) e c -> p j (e c)", j=PACK))

        def load_w_pair(q):
            pair = stream.tile([P, 2, PACK, H], BF16, name="w_raw", bufs=W_PAIR_BUFS, align_bytes=DMA_ALIGN)
            w_raw[2 * q], w_raw[2 * q + 1] = pair[:, 0], pair[:, 1]
            if q == 0:
                for a in range(2):
                    nc.sync.dma_start(out=pair[:, a], in_=wi[a].rearrange("(p j) h -> p j h", j=PACK))
            else:
                nc.sync.dma_start(out=pair[:], in_=wi[2 * q : 2 * q + 2].rearrange("e (p j) h -> p e j h", j=PACK))

        def group_x(g):
            x_grouped[g] = keep.tile([P, PACK, P, PACK], BF16, name="x_grouped%d" % g, align_bytes=64)
            src = x_raw[g][:].rearrange("p j (m t) -> p t m j", t=PACK)
            nc.vector.tensor_copy(out=x_grouped[g][:, :X_V_SLOTS], in_=src[:, :X_V_SLOTS])
            nc.scalar.copy(out=x_grouped[g][:, X_V_SLOTS:], in_=src[:, X_V_SLOTS:])

        def quant_x(g):
            x_codes[g] = keep.tile([P, M], U32, name="x_codes%d" % g, align_bytes=64)
            x_scales[g] = keep.tile([P, M], U8, name="x_scales%d" % g, align_bytes=64)
            quantize(x_codes[g][:], x_scales[g][:], x_grouped[g][:].rearrange("p t m j -> p (t m j)"))

        def group_dm(g, h):
            dm_grouped[g, h] = keep.tile([P, HALF, PACK], BF16, name="dm_grouped%d%d" % (g, h), align_bytes=64)
            src = dm_raw[g][:, :, h * HALF : (h + 1) * HALF]
            interleave(nc.vector.tensor_copy, V_RUN, dm_grouped[g, h], src, 0, DM_V_COLS)
            interleave(nc.scalar.copy, S_RUN, dm_grouped[g, h], src, DM_V_COLS, HALF)

        def quant_dm(g, h):
            dm_codes[g, h] = keep.tile([P, HALF], U32, name="dm_codes%d%d" % (g, h), align_bytes=64)
            dm_scales[g, h] = keep.tile([P, HALF], U8, name="dm_scales%d%d" % (g, h), align_bytes=64)
            quantize(dm_codes[g, h][:], dm_scales[g, h][:], dm_grouped[g, h][:].rearrange("p c j -> p (c j)"))
            ready[0] += NB // 2

        def dispatch(g, b):
            banks[g, b] = psum1.tile([P, PACK, P], BANK_DT, name="bank", tag="stage")
            h, q = divmod(b, NB // 2)
            for t in range(PACK):
                nc.tensor.matmul_mx(
                    out=banks[g, b][:, t, :],
                    lhsT=x_codes[g][:, t * P : (t + 1) * P].bitcast(FP8X4),
                    lhsT_scale=x_scales[g][:, t * P : (t + 1) * P],
                    rhs=dm_codes[g, h][:, q * P : (q + 1) * P].bitcast(FP8X4),
                    rhs_scale=dm_scales[g, h][:, q * P : (q + 1) * P],
                    start=True,
                    stop=True,
                )

        def empty_bank(g, b):
            if g == 0:
                d_grouped[b] = keep.tile([P, 2, G, C, PACK], BF16, name="d_grouped%d" % b, align_bytes=64)
            nc.scalar.copy(
                out=d_grouped[b][:, :, g, :, :],
                in_=banks[g, b][:].rearrange("p t (e c) -> p e c t", e=2),
            )

        stage1 = [(g, b) for g in range(G) for b in range(NB)]
        ready, filled, emptied = [0], [0], [0]

        def fill_next():
            if filled[0] < ready[0]:
                dispatch(*stage1[filled[0]])
                filled[0] += 1

        def empty_next(n):
            for i in range(n):
                empty_bank(*stage1[emptied[0]])
                emptied[0] += 1
                fill_next()

        def quant_d(b):
            d_codes[b] = keep.tile([P, 2 * P], U32, name="d_codes%d" % b, align_bytes=64)
            d_scales[b] = keep.tile([P, 2 * P], U8, name="d_scales%d" % b, align_bytes=64)
            quantize(d_codes[b][:], d_scales[b][:], d_grouped[b][:].rearrange("p e g c t -> p (e g c t)"))

        def lift(e):
            lifted[e] = psum1.tile([P, LIFT_COLS, PACK], BF16, name="lifted", tag="stage")
            src = w_raw[e][:, :, H - LIFT_COLS :].rearrange("p t c -> p c t")
            for c0 in range(0, LIFT_COLS, LIFT_STEP):
                c1 = min(c0 + LIFT_STEP, LIFT_COLS)
                nc.tensor.matmul(out=lifted[e][:, c0:c1, :], lhsT=ident[:], rhs=src[:, c0:c1, :], start=True, stop=True)

        def group_w(e):
            w_grouped[e] = stream.tile([P, H, PACK], BF16, name="w_grouped", align_bytes=64)
            if e < W_V_ONLY:
                interleave(nc.vector.tensor_copy, V_RUN, w_grouped[e], w_raw[e], 0, H)
                return
            interleave(nc.vector.tensor_copy, V_RUN, w_grouped[e], w_raw[e], 0, W_V_COLS)
            interleave(nc.scalar.copy, S_RUN, w_grouped[e], w_raw[e], W_V_COLS, H - LIFT_COLS)
            nc.scalar.copy(out=w_grouped[e][:, H - LIFT_COLS :, :], in_=lifted[e][:])

        def quant_w(e):
            w_codes[e] = stream.tile([P, H], U32, name="w_codes", align_bytes=64)
            w_scales[e] = stream.tile([P, H], U8, name="w_scales", align_bytes=64)
            quantize(w_codes[e][:], w_scales[e][:], w_grouped[e][:].rearrange("p c j -> p (c j)"))

        def project(e):
            b, half = e // 2, e % 2
            for n in range(H // HALF):
                accs[e, n] = psum2.tile([P, HALF], F32, name="acc")
                nc.tensor.matmul_mx(
                    out=accs[e, n][:],
                    lhsT=d_codes[b][:, half * P : (half + 1) * P].bitcast(FP8X4),
                    lhsT_scale=d_scales[b][:, half * P : (half + 1) * P],
                    rhs=w_codes[e][:, n * HALF : (n + 1) * HALF].bitcast(FP8X4),
                    rhs_scale=w_scales[e][:, n * HALF : (n + 1) * HALF],
                    start=True,
                    stop=True,
                )

        def relu_store(e):
            if e % 2 == 0:
                result_pairs[e // 2] = stream.tile([P, 2, H], F32, name="result", bufs=3, align_bytes=DMA_ALIGN)
            results[e] = result_pairs[e // 2][:, e % 2]
            rows = out[e].rearrange("g c h -> (g c) h")
            if e < E - 1:
                for n in range(H // HALF):
                    nc.scalar.activation(out=results[e][:, n * HALF : (n + 1) * HALF], in_=accs[e, n][:], func=RELU)
                if e >= PAIRED:
                    nc.sync.dma_start(out=rows, in_=results[e])
                elif e % 2 == 1:
                    nc.sync.dma_start(out=out[e - 1 : e + 1].rearrange("e g c h -> (g c) e h"), in_=result_pairs[e // 2][:])
            else:
                nc.scalar.activation(out=results[e][:, :HALF], in_=accs[e, 0][:], func=RELU)
                nc.vector.tensor_scalar_max(out=results[e][:, HALF:], in0=accs[e, 1][:], scalar1=0.0)
                nc.sync.dma_start(out=rows[:, :HALF], in_=results[e][:, :HALF])
                nc.sync.dma_start(out=rows[:, HALF:], in_=results[e][:, HALF:])

        for g in range(G):
            load_x(g)
            load_dm(g)
        for q in range(W_PAIR_BUFS):
            load_w_pair(q)

        group_x(0)
        quant_x(0)
        group_dm(0, 0)
        group_dm(0, 1)
        quant_dm(0, 0)
        for i in range(BANK_BUFS):
            fill_next()
        group_x(1)
        quant_dm(0, 1)
        empty_next(2)
        group_dm(1, 0)
        quant_x(1)
        empty_next(2)
        group_dm(1, 1)
        quant_dm(1, 0)
        empty_next(2)
        group_w(0)
        quant_dm(1, 1)
        empty_next(4)
        group_w(1)
        quant_w(0)
        empty_next(6)
        lift(2)
        for e in range(1, E):
            if e + 2 < E:
                lift(e + 2)
            if e + 1 < E:
                group_w(e + 1)
            if e % 2 == 1 and (e - 1) // 2 + W_PAIR_BUFS < E // 2:
                load_w_pair((e - 1) // 2 + W_PAIR_BUFS)
            if e == 1:
                quant_d(0)
                project(0)
            if e % 2 == 0:
                quant_d(e // 2)
            quant_w(e)
            project(e)
            relu_store(e - 1)
        relu_store(E - 1)
